import numpy as np
import ml_dtypes


def mxq(x, axis, fmt="e4m3"):
    dtype, down = {"e4m3": (ml_dtypes.float8_e4m3fn, 7), "e5m2": (ml_dtypes.float8_e5m2, 14)}[fmt]
    v = np.moveaxis(np.asarray(x, np.float32).astype(ml_dtypes.bfloat16).astype(np.float64), axis, -1)
    blocks = v.reshape(v.shape[:-1] + (-1, 32))
    amax = np.abs(blocks).max(-1, keepdims=True)
    byte = np.maximum(np.where(amax > 0, np.frexp(amax)[1] - 1 + 127, 0) - down, 1)
    scale = np.exp2(byte - 127.0)
    codes = (blocks / scale).astype(np.float32).astype(dtype).astype(np.float64)
    return np.moveaxis((codes * scale).reshape(v.shape), -1, axis)


WIDE = False


def mx_kscale(k):
    if not WIDE:
        return np.ones(k)
    levels = np.array([10, -10, 5, -5, 0])
    if k % 512:
        return np.exp2(np.random.permutation(np.resize(levels, k // 32))).repeat(32)
    a = np.empty((k // 512, 16))
    for p in range(k // 512):
        a[p, :8] = np.random.permutation(np.resize(levels, 8))
        for g in range(8):
            far = levels[np.abs(levels - a[p, g]) >= 10]
            a[p, g + 8] = far[np.random.randint(len(far))]
    return np.exp2(a.ravel()).repeat(32)


BF16 = ml_dtypes.bfloat16


def bf(x):
    return np.asarray(x, np.float32).astype(BF16)


def f64(x):
    return np.asarray(x).astype(np.float64)


B, L, M, E, H, D, FW = 1, 512, 512, 512, 8, 512, 4
EPS = 1e-5


def layer_norm(x, g, b):
    m = x.mean(-1, keepdims=True)
    v = ((x - m) ** 2).mean(-1, keepdims=True)
    return (x - m) / np.sqrt(v + EPS) * g + b


def setup_inputs():
    s, t = mx_kscale(E), mx_kscale(D)
    return {"q": bf(np.random.standard_normal((B, L, E)) * 0.5 + 0.25),
            "g1": bf((1.0 + 0.1 * np.random.standard_normal(E)) * s),
            "be1": bf(0.1 * np.random.standard_normal(E) * s),
            "Wq_s": bf(np.random.standard_normal((H, E, D)) * 1.4 / np.sqrt(E) / s[:, None] * t),
            "Wk_s": bf(np.random.standard_normal((H, E, D)) * 1.4 / np.sqrt(E) / s[:, None] / t)}


def reference(q, g1, be1, Wq_s, Wk_s):
    xq = mxq(layer_norm(f64(q), f64(g1), f64(be1)), 2, "e4m3")
    wq = mxq(f64(Wq_s).transpose(1, 0, 2).reshape(E, H * D), 0, "e4m3")
    wk = mxq(f64(Wk_s).transpose(1, 0, 2).reshape(E, H * D), 0, "e4m3")
    Q = (xq @ wq).reshape(B, L, H, D).transpose(0, 2, 1, 3)
    K = (xq @ wk).reshape(B, L, H, D).transpose(0, 2, 1, 3)
    return (mxq(Q, 3, "e4m3") @ mxq(K, 3, "e4m3").transpose(0, 1, 3, 2)) * D ** -0.5

@@ -1,0 +1,255 @@
+from contextlib import ExitStack
+
+import concourse.mybir as mybir
+from concourse.masks import make_identity
+
+F32 = mybir.dt.float32
+BF16 = mybir.dt.bfloat16
+U32 = mybir.dt.uint32
+U8 = mybir.dt.uint8
+FP8X4 = mybir.dt.float8_e4m3fn_x4
+ALU = mybir.AluOpType
+ACT = mybir.ActivationFunctionType
+
+P = 128
+PACK = 4
+L = 512
+E = 512
+D = 512
+H = 8
+LT = L // P
+HALF = L // 2
+K_SIDE, Q_SIDE = 0, 1
+EPS = 1e-5
+OUT_SCALE = D ** -0.5
+
+FLOPS = 2 * L * E * (2 * H * D) + 2 * H * L * L * D
+
+
+def regroup(copy, grouped, planes):
+    copy(
+        out=grouped.rearrange("p (c i) t -> p c t i", i=4),
+        in_=planes.rearrange("p t (c i) -> p c t i", i=4),
+    )
+
+
+def regroup_weight_columns(copy, grouped, planes):
+    copy(
+        out=grouped.rearrange("p (t g i) j -> p g t j i", t=PACK, i=4),
+        in_=planes.rearrange("p j (g t i) -> p g t j i", t=PACK, i=4),
+    )
+
+
+def tile_decoderlayer_pb_kernel(tc, q, g1, be1, Wq_s, Wk_s, out):
+    nc = tc.nc
+    with ExitStack() as ctx:
+        const = ctx.enter_context(tc.tile_pool(name="const", bufs=1))
+        norm = ctx.enter_context(tc.tile_pool(name="norm", bufs=1))
+        raw_pool = ctx.enter_context(tc.tile_pool(name="raw", bufs=1))
+        wg_pool = ctx.enter_context(tc.tile_pool(name="wg", bufs=2))
+        wc_pool = ctx.enter_context(tc.tile_pool(name="wc", bufs=3))
+        qk_pool = ctx.enter_context(tc.tile_pool(name="qk", bufs=3))
+        out_pool = ctx.enter_context(tc.tile_pool(name="outp", bufs=16))
+        psum = ctx.enter_context(tc.psum_pool(name="psum", bufs=8))
+
+        q_sb = norm.tile([P, LT, E], BF16)
+        q_rows = q.flatten_outer_dims().rearrange("(lt p) e -> lt p e", p=P)
+        for lt in range(LT):
+            nc.sync.dma_start(out=q_sb[:, lt, :], in_=q_rows[lt])
+        g_bf = norm.tile([P, PACK], BF16)
+        nc.sync.dma_start(out=g_bf[:], in_=g1.rearrange("(p t) -> p t", t=PACK))
+        b_bf = norm.tile([P, PACK], BF16)
+        nc.sync.dma_start(out=b_bf[:], in_=be1.rearrange("(p t) -> p t", t=PACK))
+        w_raw = []
+        for h in range(H):
+            raw = raw_pool.tile([P, 2, PACK, D], BF16, name="w_raw%d" % h)
+            nc.sync.dma_start(out=raw[:, K_SIDE], in_=Wk_s[h, :, :].rearrange("(p t) d -> p t d", t=PACK))
+            nc.sync.dma_start(out=raw[:, Q_SIDE], in_=Wq_s[h, :, :].rearrange("(p t) d -> p t d", t=PACK))
+            w_raw.append(raw)
+
+        ident = const.tile([P, P], F32)
+        make_identity(nc, ident[:])
+        eps_t = const.tile([P, 1], F32)
+        nc.vector.memset(eps_t[:], EPS)
+        warm = const.tile([P, 1], F32)
+        nc.scalar.activation(out=warm[:], in_=eps_t[:], func=ACT.Sqrt)
+
+        w_codes = {}
+        w_scales = {}
+
+        w_grouped = {}
+
+        def regroup_weights(copy, h, side):
+            if side == K_SIDE:
+                w_grouped[h] = wg_pool.tile([P, 2, D, PACK], BF16, align_bytes=64, name="w_grouped")
+            regroup_weight_columns(copy, w_grouped[h][:, side], w_raw[h][:, side])
+
+        def quantise_weights(h, first_side, n_sides):
+            if first_side == K_SIDE:
+                w_codes[h] = wc_pool.tile([P, 2 * D], U32, align_bytes=64, name="w_codes")
+                w_scales[h] = wc_pool.tile([P, 2 * D], U8, align_bytes=64, name="w_scales")
+            cols = slice(first_side * D, (first_side + n_sides) * D)
+            nc.vector.quantize_mx(
+                out=w_codes[h][:, cols].bitcast(FP8X4),
+                scales=w_scales[h][:, cols],
+                in_=w_grouped[h][:, first_side : first_side + n_sides].rearrange("p s d t -> p (s d t)"),
+            )
+
+        stats = norm.tile([P, LT, 6], F32)
+        mean_var = norm.tile([P, LT, 2], F32)
+        std = norm.tile([P, LT], F32)
+        rstd = norm.tile([P, LT], F32)
+        shift = norm.tile([P, LT], F32)
+        g_f = norm.tile([P, PACK], F32)
+        b_f = norm.tile([P, PACK], F32)
+        xhat = norm.tile([P, LT, PACK, P], F32)
+        xT_banks = []
+        for half in range(2):
+            four = []
+            for t in range(PACK):
+                xT_bank = psum.tile([P, HALF], F32, tag="bank", name="xT_bank%d%d" % (half, t))
+                four.append(xT_bank)
+            xT_banks.append(four)
+
+        def statistics(lt):
+            nc.vector.bn_stats(out=stats[:, lt, :], in_=q_sb[:, lt, :])
+            nc.vector.bn_aggr(out=mean_var[:, lt, :], in_=stats[:, lt, :])
+            nc.scalar.activation(
+                out=std[:, lt : lt + 1], in_=mean_var[:, lt, 1:2], func=ACT.Sqrt, bias=eps_t[:, 0:1], scale=1.0
+            )
+
+        def normalise(lt):
+            nc.vector.reciprocal(out=rstd[:, lt : lt + 1], in_=std[:, lt : lt + 1])
+            nc.vector.scalar_tensor_tensor(
+                out=shift[:, lt : lt + 1], in0=mean_var[:, lt, 0:1], scalar=-1.0, in1=rstd[:, lt : lt + 1],
+                op0=ALU.mult, op1=ALU.mult,
+            )
+            nc.scalar.activation(
+                out=xhat[:, lt], in_=q_sb[:, lt, :].rearrange("p (j t) -> p t j", t=PACK), func=ACT.Identity,
+                scale=rstd[:, lt : lt + 1], bias=shift[:, lt : lt + 1],
+            )
+            l_cols = slice((lt % 2) * P, (lt % 2 + 1) * P)
+            for t in range(PACK):
+                nc.tensor.transpose(out=xT_banks[lt // 2][t][:, l_cols], in_=xhat[:, lt, t, :], identity=ident[:])
+
+        x_planes = norm.tile([P, PACK, L], BF16)
+        x_grouped = norm.tile([P, L, PACK], BF16, align_bytes=64)
+        x_codes = norm.tile([P, L], U32, align_bytes=64)
+        x_scales = norm.tile([P, L], U8, align_bytes=64)
+
+        def scale_and_shift(half):
+            l_cols = slice(half * HALF, (half + 1) * HALF)
+            for t in range(PACK):
+                if t % 2 == 0:
+                    nc.vector.tensor_scalar(
+                        out=x_planes[:, t, l_cols], in0=xT_banks[half][t][:],
+                        scalar1=g_f[:, t : t + 1], scalar2=b_f[:, t : t + 1], op0=ALU.mult, op1=ALU.add,
+                    )
+                else:
+                    nc.scalar.activation(
+                        out=x_planes[:, t, l_cols], in_=xT_banks[half][t][:], func=ACT.Identity,
+                        scale=g_f[:, t : t + 1], bias=b_f[:, t : t + 1],
+                    )
+
+        def regroup_x(half):
+            l_cols = slice(half * HALF, (half + 1) * HALF)
+            regroup(nc.vector.tensor_copy, x_grouped[:, l_cols, :], x_planes[:, :, l_cols])
+
+        def quantise_x(half):
+            l_cols = slice(half * HALF, (half + 1) * HALF)
+            nc.vector.quantize_mx(
+                out=x_codes[:, l_cols].bitcast(FP8X4),
+                scales=x_scales[:, l_cols],
+                in_=x_grouped[:, l_cols, :].rearrange("p l t -> p (l t)"),
+            )
+
+        statistics(0)
+        for lt in range(1, LT):
+            statistics(lt)
+            normalise(lt - 1)
+        nc.gpsimd.tensor_copy(out=g_f[:], in_=g_bf[:])
+        nc.gpsimd.tensor_copy(out=b_f[:], in_=b_bf[:])
+        normalise(LT - 1)
+
+        regroup_weights(nc.vector.tensor_copy, 0, K_SIDE)
+        scale_and_shift(0)
+        quantise_weights(0, K_SIDE, 1)
+        regroup_x(0)
+        scale_and_shift(1)
+        regroup_weights(nc.scalar.copy, 0, Q_SIDE)
+        quantise_x(0)
+        regroup_x(1)
+        quantise_x(1)
+        quantise_weights(0, Q_SIDE, 1)
+
+        qk_grouped = {}
+        qk_codes = {}
+        qk_scales = {}
+
+        def prepare_weights(h):
+            for side in range(2):
+                regroup_weights(nc.vector.tensor_copy, h, side)
+            quantise_weights(h, K_SIDE, 2)
+
+        def project(h, side):
+            if side == K_SIDE:
+                qk_grouped[h] = qk_pool.tile([P, 2, L, PACK], BF16, align_bytes=64, name="qk_grouped")
+                qk_codes[h] = qk_pool.tile([P, 2 * L], U32, align_bytes=64, name="qk_codes")
+                qk_scales[h] = qk_pool.tile([P, 2 * L], U8, align_bytes=64, name="qk_scales")
+            for lb in range(LT):
+                l_cols = slice(lb * P, (lb + 1) * P)
+                bank = psum.tile([P, PACK, P], F32, tag="bank", name="proj_bank")
+                for t in range(PACK):
+                    d_cols = slice(side * D + t * P, side * D + (t + 1) * P)
+                    nc.tensor.matmul_mx(
+                        out=bank[:, t, :],
+                        lhsT=w_codes[h][:, d_cols].bitcast(FP8X4),
+                        lhsT_scale=w_scales[h][:, d_cols],
+                        rhs=x_codes[:, l_cols].bitcast(FP8X4),
+                        rhs_scale=x_scales[:, l_cols],
+                        start=True,
+                        stop=True,
+                    )
+                if h == H - 1 and lb == LT - 1:
+                    copy = nc.vector.tensor_copy
+                else:
+                    copy = nc.scalar.copy
+                copy(out=qk_grouped[h][:, side, l_cols, :], in_=bank[:].rearrange("p t l -> p l t"))
+                if lb % 2 == 1:
+                    half_l = slice((lb - 1) * P, (lb + 1) * P)
+                    half_cols = slice(side * L + (lb - 1) * P, side * L + (lb + 1) * P)
+                    nc.vector.quantize_mx(
+                        out=qk_codes[h][:, half_cols].bitcast(FP8X4),
+                        scales=qk_scales[h][:, half_cols],
+                        in_=qk_grouped[h][:, side, half_l, :].rearrange("p l t -> p (l t)"),
+                    )
+
+        def logits(h):
+            k_cols = slice(K_SIDE * L, (K_SIDE + 1) * L)
+            for lt in range(LT):
+                q_cols = slice(Q_SIDE * L + lt * P, Q_SIDE * L + (lt + 1) * P)
+                bank = psum.tile([P, L], F32, tag="bank", name="logit_bank")
+                nc.tensor.matmul_mx(
+                    out=bank[:],
+                    lhsT=qk_codes[h][:, q_cols].bitcast(FP8X4),
+                    lhsT_scale=qk_scales[h][:, q_cols],
+                    rhs=qk_codes[h][:, k_cols].bitcast(FP8X4),
+                    rhs_scale=qk_scales[h][:, k_cols],
+                    start=True,
+                    stop=True,
+                )
+                rows = out_pool.tile([P, L], F32, name="out_rows")
+                if lt % 2 == 0:
+                    nc.scalar.mul(out=rows[:], in_=bank[:], mul=OUT_SCALE)
+                else:
+                    nc.vector.tensor_scalar(out=rows[:], in0=bank[:], scalar1=OUT_SCALE, scalar2=None, op0=ALU.mult)
+                nc.sync.dma_start(out=out[0, h, lt * P : (lt + 1) * P, :], in_=rows[:])
+
+        for h in range(H):
+            if h + 1 < H:
+                prepare_weights(h + 1)
+            project(h, K_SIDE)
+            if h > 0:
+                logits(h - 1)
+            project(h, Q_SIDE)
+        logits(H - 1)

@@ -189,7 +189,8 @@ def tile_decoderlayer_pb_kernel(tc, q, g1, be1, Wq_s, Wk_s, out):
         def prepare_weights(h):
             for side in range(2):
                 regroup_weights(nc.vector.tensor_copy, h, side)
-            quantise_weights(h, K_SIDE, 2)
+            for side in range(2):
+                quantise_weights(h, side, 1)
 
         def project(h, side):
             if side == K_SIDE:

@@ -48,9 +48,9 @@ def tile_decoderlayer_pb_kernel(tc, q, g1, be1, Wq_s, Wk_s, out):
         raw_pool = ctx.enter_context(tc.tile_pool(name="raw", bufs=1))
         wg_pool = ctx.enter_context(tc.tile_pool(name="wg", bufs=2))
         wc_pool = ctx.enter_context(tc.tile_pool(name="wc", bufs=3))
-        qk_pool = ctx.enter_context(tc.tile_pool(name="qk", bufs=3))
+        qk_pool = ctx.enter_context(tc.tile_pool(name="qk", bufs=6))
         out_pool = ctx.enter_context(tc.tile_pool(name="outp", bufs=16))
-        psum = ctx.enter_context(tc.psum_pool(name="psum", bufs=8))
+        psum = ctx.enter_context(tc.psum_pool(name="psum", bufs=1))
 
         q_sb = norm.tile([P, LT, E], BF16)
         q_rows = q.flatten_outer_dims().rearrange("(lt p) e -> lt p e", p=P)
@@ -79,10 +79,16 @@ def tile_decoderlayer_pb_kernel(tc, q, g1, be1, Wq_s, Wk_s, out):
 
         w_grouped = {}
 
-        def regroup_weights(copy, h, side):
-            if side == K_SIDE:
+        def regroup_weights(copy, h, side, first=0, last=None, pieces=1):
+            if side == K_SIDE and first == 0:
                 w_grouped[h] = wg_pool.tile([P, 2, D, PACK], BF16, align_bytes=64, name="w_grouped")
-            regroup_weight_columns(copy, w_grouped[h][:, side], w_raw[h][:, side])
+            width = D // 16 // pieces
+            for piece in range(first, pieces if last is None else last):
+                groups = slice(piece * width, (piece + 1) * width)
+                copy(
+                    out=w_grouped[h][:, side].rearrange("p (t g i) j -> p g t j i", t=PACK, i=4)[:, groups],
+                    in_=w_raw[h][:, side].rearrange("p j (g t i) -> p g t j i", t=PACK, i=4)[:, groups],
+                )
 
         def quantise_weights(h, first_side, n_sides):
             if first_side == K_SIDE:
@@ -105,32 +111,61 @@ def tile_decoderlayer_pb_kernel(tc, q, g1, be1, Wq_s, Wk_s, out):
         xhat = norm.tile([P, LT, PACK, P], F32)
         xT_banks = []
         for half in range(2):
-            four = []
-            for t in range(PACK):
-                xT_bank = psum.tile([P, HALF], F32, tag="bank", name="xT_bank%d%d" % (half, t))
-                four.append(xT_bank)
-            xT_banks.append(four)
+            even_bank = psum.tile([P, 2, HALF], F32, tag="vector_bank", bufs=2, name="xT_even%d" % half)
+            odd_bank = psum.tile([P, 2, HALF], F32, tag="scalar_bank", bufs=6, name="xT_odd%d" % half)
+            xT_banks.append((even_bank, odd_bank))
 
-        def statistics(lt):
+        total = norm.tile([P, 1], F32)
+        squares = norm.tile([P, 1], F32)
+        neg_mean = norm.tile([P, 1], F32)
+        waste_sum = norm.tile([P, E], F32)
+        waste_squares = norm.tile([P, E], F32)
+        std_1 = norm.tile([P, 1], F32)
+        rstd_1 = norm.tile([P, 1], F32)
+        shift_1 = norm.tile([P, 1], F32)
+
+        def vector_statistics(lt):
             nc.vector.bn_stats(out=stats[:, lt, :], in_=q_sb[:, lt, :])
+
+        def vector_moments(lt):
             nc.vector.bn_aggr(out=mean_var[:, lt, :], in_=stats[:, lt, :])
             nc.scalar.activation(
                 out=std[:, lt : lt + 1], in_=mean_var[:, lt, 1:2], func=ACT.Sqrt, bias=eps_t[:, 0:1], scale=1.0
             )
 
-        def normalise(lt):
+        def vector_shift(lt):
             nc.vector.reciprocal(out=rstd[:, lt : lt + 1], in_=std[:, lt : lt + 1])
             nc.vector.scalar_tensor_tensor(
                 out=shift[:, lt : lt + 1], in0=mean_var[:, lt, 0:1], scalar=-1.0, in1=rstd[:, lt : lt + 1],
                 op0=ALU.mult, op1=ALU.mult,
             )
+
+        def scalar_sum():
+            nc.scalar.activation(out=waste_sum[:], in_=q_sb[:, 1, :], func=ACT.Identity, accum_out=total[:])
+            nc.scalar.mul(out=neg_mean[:], in_=total[:], mul=-1.0 / E)
+
+        def scalar_squares():
+            nc.scalar.activation(
+                out=waste_squares[:], in_=q_sb[:, 1, :], func=ACT.Square, bias=neg_mean[:, 0:1], accum_out=squares[:]
+            )
+            nc.scalar.activation(out=std_1[:], in_=squares[:], func=ACT.Sqrt, bias=eps_t[:, 0:1], scale=1.0 / E)
+
+        def scalar_shift():
+            nc.vector.reciprocal(out=rstd_1[:], in_=std_1[:])
+            nc.scalar.activation(out=shift_1[:], in_=neg_mean[:], func=ACT.Copy, scale=rstd_1[:, 0:1])
+
+        def normalise(lt):
+            if lt == 1:
+                scale, bias = rstd_1[:, 0:1], shift_1[:, 0:1]
+            else:
+                scale, bias = rstd[:, lt : lt + 1], shift[:, lt : lt + 1]
             nc.scalar.activation(
                 out=xhat[:, lt], in_=q_sb[:, lt, :].rearrange("p (j t) -> p t j", t=PACK), func=ACT.Identity,
-                scale=rstd[:, lt : lt + 1], bias=shift[:, lt : lt + 1],
+                scale=scale, bias=bias,
             )
             l_cols = slice((lt % 2) * P, (lt % 2 + 1) * P)
             for t in range(PACK):
-                nc.tensor.transpose(out=xT_banks[lt // 2][t][:, l_cols], in_=xhat[:, lt, t, :], identity=ident[:])
+                nc.tensor.transpose(out=xT_banks[lt // 2][t % 2][:, t // 2, l_cols], in_=xhat[:, lt, t, :], identity=ident[:])
 
         x_planes = norm.tile([P, PACK, L], BF16)
         x_grouped = norm.tile([P, L, PACK], BF16, align_bytes=64)
@@ -140,14 +175,14 @@ def tile_decoderlayer_pb_kernel(tc, q, g1, be1, Wq_s, Wk_s, out):
         def scale_and_shift(half):
             l_cols = slice(half * HALF, (half + 1) * HALF)
             for t in range(PACK):
-                if t % 2 == 0:
+                if half == 0 and t % 2 == 0:
                     nc.vector.tensor_scalar(
-                        out=x_planes[:, t, l_cols], in0=xT_banks[half][t][:],
+                        out=x_planes[:, t, l_cols], in0=xT_banks[half][t % 2][:, t // 2, :],
                         scalar1=g_f[:, t : t + 1], scalar2=b_f[:, t : t + 1], op0=ALU.mult, op1=ALU.add,
                     )
                 else:
                     nc.scalar.activation(
-                        out=x_planes[:, t, l_cols], in_=xT_banks[half][t][:], func=ACT.Identity,
+                        out=x_planes[:, t, l_cols], in_=xT_banks[half][t % 2][:, t // 2, :], func=ACT.Identity,
                         scale=g_f[:, t : t + 1], bias=b_f[:, t : t + 1],
                     )
 
@@ -163,94 +198,141 @@ def tile_decoderlayer_pb_kernel(tc, q, g1, be1, Wq_s, Wk_s, out):
                 in_=x_grouped[:, l_cols, :].rearrange("p l t -> p (l t)"),
             )
 
-        statistics(0)
-        for lt in range(1, LT):
-            statistics(lt)
-            normalise(lt - 1)
         nc.gpsimd.tensor_copy(out=g_f[:], in_=g_bf[:])
         nc.gpsimd.tensor_copy(out=b_f[:], in_=b_bf[:])
-        normalise(LT - 1)
-
-        regroup_weights(nc.vector.tensor_copy, 0, K_SIDE)
-        scale_and_shift(0)
-        quantise_weights(0, K_SIDE, 1)
-        regroup_x(0)
-        scale_and_shift(1)
-        regroup_weights(nc.scalar.copy, 0, Q_SIDE)
-        quantise_x(0)
-        regroup_x(1)
-        quantise_x(1)
-        quantise_weights(0, Q_SIDE, 1)
 
         qk_grouped = {}
         qk_codes = {}
         qk_scales = {}
 
-        def prepare_weights(h):
-            for side in range(2):
-                regroup_weights(nc.vector.tensor_copy, h, side)
-            for side in range(2):
-                quantise_weights(h, side, 1)
+        def take_bank(on_vector, shape, name):
+            if on_vector:
+                bank = psum.tile(shape, F32, tag="vector_bank", bufs=2, name=name)
+            else:
+                bank = psum.tile(shape, F32, tag="scalar_bank", bufs=6, name=name)
+            return bank
 
-        def project(h, side):
-            if side == K_SIDE:
-                qk_grouped[h] = qk_pool.tile([P, 2, L, PACK], BF16, align_bytes=64, name="qk_grouped")
-                qk_codes[h] = qk_pool.tile([P, 2 * L], U32, align_bytes=64, name="qk_codes")
-                qk_scales[h] = qk_pool.tile([P, 2 * L], U8, align_bytes=64, name="qk_scales")
-            for lb in range(LT):
-                l_cols = slice(lb * P, (lb + 1) * P)
-                bank = psum.tile([P, PACK, P], F32, tag="bank", name="proj_bank")
-                for t in range(PACK):
-                    d_cols = slice(side * D + t * P, side * D + (t + 1) * P)
-                    nc.tensor.matmul_mx(
-                        out=bank[:, t, :],
-                        lhsT=w_codes[h][:, d_cols].bitcast(FP8X4),
-                        lhsT_scale=w_scales[h][:, d_cols],
-                        rhs=x_codes[:, l_cols].bitcast(FP8X4),
-                        rhs_scale=x_scales[:, l_cols],
-                        start=True,
-                        stop=True,
-                    )
-                if h == H - 1 and lb == LT - 1:
-                    copy = nc.vector.tensor_copy
-                else:
-                    copy = nc.scalar.copy
-                copy(out=qk_grouped[h][:, side, l_cols, :], in_=bank[:].rearrange("p t l -> p l t"))
-                if lb % 2 == 1:
-                    half_l = slice((lb - 1) * P, (lb + 1) * P)
-                    half_cols = slice(side * L + (lb - 1) * P, side * L + (lb + 1) * P)
-                    nc.vector.quantize_mx(
-                        out=qk_codes[h][:, half_cols].bitcast(FP8X4),
-                        scales=qk_scales[h][:, half_cols],
-                        in_=qk_grouped[h][:, side, half_l, :].rearrange("p l t -> p (l t)"),
-                    )
-
-        def logits(h):
-            k_cols = slice(K_SIDE * L, (K_SIDE + 1) * L)
-            for lt in range(LT):
-                q_cols = slice(Q_SIDE * L + lt * P, Q_SIDE * L + (lt + 1) * P)
-                bank = psum.tile([P, L], F32, tag="bank", name="logit_bank")
+        def project(h, side, lb, on_vector=False):
+            if lb == 0:
+                qk_grouped[h, side] = qk_pool.tile([P, L, PACK], BF16, align_bytes=64, name="qk_grouped")
+                qk_codes[h, side] = qk_pool.tile([P, L], U32, align_bytes=64, name="qk_codes")
+                qk_scales[h, side] = qk_pool.tile([P, L], U8, align_bytes=64, name="qk_scales")
+            l_cols = slice(lb * P, (lb + 1) * P)
+            bank = take_bank(on_vector, [P, PACK, P], "proj_bank")
+            for t in range(PACK):
+                d_cols = slice(side * D + t * P, side * D + (t + 1) * P)
                 nc.tensor.matmul_mx(
-                    out=bank[:],
-                    lhsT=qk_codes[h][:, q_cols].bitcast(FP8X4),
-                    lhsT_scale=qk_scales[h][:, q_cols],
-                    rhs=qk_codes[h][:, k_cols].bitcast(FP8X4),
-                    rhs_scale=qk_scales[h][:, k_cols],
+                    out=bank[:, t, :],
+                    lhsT=w_codes[h][:, d_cols].bitcast(FP8X4),
+                    lhsT_scale=w_scales[h][:, d_cols],
+                    rhs=x_codes[:, l_cols].bitcast(FP8X4),
+                    rhs_scale=x_scales[:, l_cols],
                     start=True,
                     stop=True,
                 )
-                rows = out_pool.tile([P, L], F32, name="out_rows")
-                if lt % 2 == 0:
-                    nc.scalar.mul(out=rows[:], in_=bank[:], mul=OUT_SCALE)
-                else:
-                    nc.vector.tensor_scalar(out=rows[:], in0=bank[:], scalar1=OUT_SCALE, scalar2=None, op0=ALU.mult)
-                nc.sync.dma_start(out=out[0, h, lt * P : (lt + 1) * P, :], in_=rows[:])
+            copy = nc.vector.tensor_copy if on_vector else nc.scalar.copy
+            copy(out=qk_grouped[h, side][:, l_cols, :], in_=bank[:].rearrange("p t l -> p l t"))
 
-        for h in range(H):
-            if h + 1 < H:
-                prepare_weights(h + 1)
-            project(h, K_SIDE)
-            if h > 0:
-                logits(h - 1)
-            project(h, Q_SIDE)
-        logits(H - 1)
+        def quantise_qk(h, side, half):
+            l_cols = slice(half * HALF, (half + 1) * HALF)
+            nc.vector.quantize_mx(
+                out=qk_codes[h, side][:, l_cols].bitcast(FP8X4),
+                scales=qk_scales[h, side][:, l_cols],
+                in_=qk_grouped[h, side][:, l_cols, :].rearrange("p l t -> p (l t)"),
+            )
+
+        def logits(h, lt, on_vector):
+            q_cols = slice(lt * P, (lt + 1) * P)
+            bank = take_bank(on_vector, [P, L], "logit_bank")
+            nc.tensor.matmul_mx(
+                out=bank[:],
+                lhsT=qk_codes[h, Q_SIDE][:, q_cols].bitcast(FP8X4),
+                lhsT_scale=qk_scales[h, Q_SIDE][:, q_cols],
+                rhs=qk_codes[h, K_SIDE][:].bitcast(FP8X4),
+                rhs_scale=qk_scales[h, K_SIDE][:],
+                start=True,
+                stop=True,
+            )
+            rows = out_pool.tile([P, L], F32, name="out_rows")
+            if on_vector:
+                nc.vector.tensor_scalar(out=rows[:], in0=bank[:], scalar1=OUT_SCALE, scalar2=None, op0=ALU.mult)
+            else:
+                nc.scalar.mul(out=rows[:], in_=bank[:], mul=OUT_SCALE)
+            nc.sync.dma_start(out=out[0, h, lt * P : (lt + 1) * P, :], in_=rows[:])
+
+        ctx.enter_context(tc.manual_schedule())
+        vector_statistics(0)
+        scalar_sum()
+        vector_moments(0)
+        scalar_squares()
+        vector_statistics(2)
+        vector_shift(0)
+        vector_moments(2)
+        normalise(0)
+        vector_statistics(3)
+        scalar_shift()
+        normalise(1)
+        vector_moments(3)
+        vector_shift(2)
+        normalise(2)
+        regroup_weights(nc.vector.tensor_copy, 0, K_SIDE, first=0, last=1, pieces=2)
+        vector_shift(3)
+        normalise(3)
+        regroup_weights(nc.vector.tensor_copy, 0, K_SIDE, first=1, last=2, pieces=2)
+        scale_and_shift(0)
+        regroup_x(0)
+        quantise_weights(0, K_SIDE, 1)
+        quantise_x(0)
+        scale_and_shift(1)
+        regroup_weights(nc.scalar.copy, 0, Q_SIDE, first=0, last=2, pieces=4)
+        project(0, K_SIDE, 0)
+        project(0, K_SIDE, 1)
+        regroup_x(1)
+        regroup_weights(nc.vector.tensor_copy, 0, Q_SIDE, first=2, last=3, pieces=4)
+        quantise_x(1)
+        regroup_weights(nc.vector.tensor_copy, 0, Q_SIDE, first=3, last=4, pieces=4)
+        project(0, K_SIDE, 2)
+        project(0, K_SIDE, 3)
+        quantise_weights(0, Q_SIDE, 1)
+        for lb in range(LT):
+            project(0, Q_SIDE, lb)
+        regroup_weights(nc.vector.tensor_copy, 1, K_SIDE)
+        quantise_qk(0, K_SIDE, 0)
+        quantise_weights(1, K_SIDE, 1)
+        quantise_qk(0, K_SIDE, 1)
+        regroup_weights(nc.vector.tensor_copy, 1, Q_SIDE)
+        quantise_qk(0, Q_SIDE, 0)
+        quantise_weights(1, Q_SIDE, 1)
+        quantise_qk(0, Q_SIDE, 1)
+
+        for h in range(1, H - 1):
+            for lb in range(LT):
+                project(h, K_SIDE, lb)
+            regroup_weights(nc.vector.tensor_copy, h + 1, K_SIDE)
+            quantise_qk(h, K_SIDE, 0)
+            quantise_weights(h + 1, K_SIDE, 1)
+            quantise_qk(h, K_SIDE, 1)
+            for lb in range(LT):
+                project(h, Q_SIDE, lb)
+            regroup_weights(nc.vector.tensor_copy, h + 1, Q_SIDE)
+            quantise_qk(h, Q_SIDE, 0)
+            quantise_weights(h + 1, Q_SIDE, 1)
+            quantise_qk(h, Q_SIDE, 1)
+            for lt in range(LT):
+                logits(h - 1, lt, lt == 3 or (lt == 1 and h > 2))
+
+        for lb in range(LT):
+            project(H - 1, K_SIDE, lb)
+        quantise_qk(H - 1, K_SIDE, 0)
+        quantise_qk(H - 1, K_SIDE, 1)
+        for lt in (0, 1):
+            logits(H - 2, lt, lt == 1)
+
+        for lb in range(LT):
+            project(H - 1, Q_SIDE, lb, on_vector=lb % 2 == 1)
+            if lb % 2 == 1:
+                quantise_qk(H - 1, Q_SIDE, lb // 2)
+        for lt in (2, 3):
+            logits(H - 2, lt, False)
+        for lt in range(LT):
+            logits(H - 1, lt, lt % 2 == 1)

@@ -19,6 +19,7 @@ D = 512
 H = 8
 LT = L // P
 HALF = L // 2
+RUN = 8
 K_SIDE, Q_SIDE = 0, 1
 EPS = 1e-5
 OUT_SCALE = D ** -0.5
@@ -30,13 +31,6 @@ def regroup(copy, grouped, planes):
     copy(
         out=grouped.rearrange("p (c i) t -> p c t i", i=4),
         in_=planes.rearrange("p t (c i) -> p c t i", i=4),
-    )
-
-
-def regroup_weight_columns(copy, grouped, planes):
-    copy(
-        out=grouped.rearrange("p (t g i) j -> p g t j i", t=PACK, i=4),
-        in_=planes.rearrange("p j (g t i) -> p g t j i", t=PACK, i=4),
     )
 
 
@@ -82,12 +76,12 @@ def tile_decoderlayer_pb_kernel(tc, q, g1, be1, Wq_s, Wk_s, out):
         def regroup_weights(copy, h, side, first=0, last=None, pieces=1):
             if side == K_SIDE and first == 0:
                 w_grouped[h] = wg_pool.tile([P, 2, D, PACK], BF16, align_bytes=64, name="w_grouped")
-            width = D // 16 // pieces
+            width = D // (PACK * RUN) // pieces
             for piece in range(first, pieces if last is None else last):
                 groups = slice(piece * width, (piece + 1) * width)
                 copy(
-                    out=w_grouped[h][:, side].rearrange("p (t g i) j -> p g t j i", t=PACK, i=4)[:, groups],
-                    in_=w_raw[h][:, side].rearrange("p j (g t i) -> p g t j i", t=PACK, i=4)[:, groups],
+                    out=w_grouped[h][:, side].rearrange("p (t g i) j -> p g t j i", t=PACK, i=RUN)[:, groups],
+                    in_=w_raw[h][:, side].rearrange("p j (g t i) -> p g t j i", t=PACK, i=RUN)[:, groups],
                 )
 
         def quantise_weights(h, first_side, n_sides):

@@ -313,7 +313,7 @@ def tile_decoderlayer_pb_kernel(tc, q, g1, be1, Wq_s, Wk_s, out):
             quantise_weights(h + 1, Q_SIDE, 1)
             quantise_qk(h, Q_SIDE, 1)
             for lt in range(LT):
-                logits(h - 1, lt, lt == 3 or (lt == 1 and h > 2))
+                logits(h - 1, lt, lt == 3 or (lt == 1 and h > 1))
 
         for lb in range(LT):
             project(H - 1, K_SIDE, lb)

from contextlib import ExitStack

import concourse.mybir as mybir
from concourse.masks import make_identity

F32 = mybir.dt.float32
BF16 = mybir.dt.bfloat16
U32 = mybir.dt.uint32
U8 = mybir.dt.uint8
FP8X4 = mybir.dt.float8_e4m3fn_x4
ALU = mybir.AluOpType
ACT = mybir.ActivationFunctionType

P = 128
PACK = 4
L = 512
E = 512
D = 512
H = 8
LT = L // P
HALF = L // 2
RUN = 8
K_SIDE, Q_SIDE = 0, 1
EPS = 1e-5
OUT_SCALE = D ** -0.5

FLOPS = 2 * L * E * (2 * H * D) + 2 * H * L * L * D


def regroup(copy, grouped, planes):
    copy(
        out=grouped.rearrange("p (c i) t -> p c t i", i=4),
        in_=planes.rearrange("p t (c i) -> p c t i", i=4),
    )


def tile_decoderlayer_pb_kernel(tc, q, g1, be1, Wq_s, Wk_s, out):
    nc = tc.nc
    with ExitStack() as ctx:
        const = ctx.enter_context(tc.tile_pool(name="const", bufs=1))
        norm = ctx.enter_context(tc.tile_pool(name="norm", bufs=1))
        raw_pool = ctx.enter_context(tc.tile_pool(name="raw", bufs=1))
        wg_pool = ctx.enter_context(tc.tile_pool(name="wg", bufs=2))
        wc_pool = ctx.enter_context(tc.tile_pool(name="wc", bufs=3))
        qk_pool = ctx.enter_context(tc.tile_pool(name="qk", bufs=6))
        out_pool = ctx.enter_context(tc.tile_pool(name="outp", bufs=16))
        psum = ctx.enter_context(tc.psum_pool(name="psum", bufs=1))

        q_sb = norm.tile([P, LT, E], BF16)
        q_rows = q.flatten_outer_dims().rearrange("(lt p) e -> lt p e", p=P)
        for lt in range(LT):
            nc.sync.dma_start(out=q_sb[:, lt, :], in_=q_rows[lt])
        g_bf = norm.tile([P, PACK], BF16)
        nc.sync.dma_start(out=g_bf[:], in_=g1.rearrange("(p t) -> p t", t=PACK))
        b_bf = norm.tile([P, PACK], BF16)
        nc.sync.dma_start(out=b_bf[:], in_=be1.rearrange("(p t) -> p t", t=PACK))
        w_raw = []
        for h in range(H):
            raw = raw_pool.tile([P, 2, PACK, D], BF16, name="w_raw%d" % h)
            nc.sync.dma_start(out=raw[:, K_SIDE], in_=Wk_s[h, :, :].rearrange("(p t) d -> p t d", t=PACK))
            nc.sync.dma_start(out=raw[:, Q_SIDE], in_=Wq_s[h, :, :].rearrange("(p t) d -> p t d", t=PACK))
            w_raw.append(raw)

        ident = const.tile([P, P], F32)
        make_identity(nc, ident[:])
        eps_t = const.tile([P, 1], F32)
        nc.vector.memset(eps_t[:], EPS)
        warm = const.tile([P, 1], F32)
        nc.scalar.activation(out=warm[:], in_=eps_t[:], func=ACT.Sqrt)

        w_codes = {}
        w_scales = {}

        w_grouped = {}

        def regroup_weights(copy, h, side, first=0, last=None, pieces=1):
            if side == K_SIDE and first == 0:
                w_grouped[h] = wg_pool.tile([P, 2, D, PACK], BF16, align_bytes=64, name="w_grouped")
            width = D // (PACK * RUN) // pieces
            for piece in range(first, pieces if last is None else last):
                groups = slice(piece * width, (piece + 1) * width)
                copy(
                    out=w_grouped[h][:, side].rearrange("p (t g i) j -> p g t j i", t=PACK, i=RUN)[:, groups],
                    in_=w_raw[h][:, side].rearrange("p j (g t i) -> p g t j i", t=PACK, i=RUN)[:, groups],
                )

        def quantise_weights(h, first_side, n_sides):
            if first_side == K_SIDE:
                w_codes[h] = wc_pool.tile([P, 2 * D], U32, align_bytes=64, name="w_codes")
                w_scales[h] = wc_pool.tile([P, 2 * D], U8, align_bytes=64, name="w_scales")
            cols = slice(first_side * D, (first_side + n_sides) * D)
            nc.vector.quantize_mx(
                out=w_codes[h][:, cols].bitcast(FP8X4),
                scales=w_scales[h][:, cols],
                in_=w_grouped[h][:, first_side : first_side + n_sides].rearrange("p s d t -> p (s d t)"),
            )

        stats = norm.tile([P, LT, 6], F32)
        mean_var = norm.tile([P, LT, 2], F32)
        std = norm.tile([P, LT], F32)
        rstd = norm.tile([P, LT], F32)
        shift = norm.tile([P, LT], F32)
        g_f = norm.tile([P, PACK], F32)
        b_f = norm.tile([P, PACK], F32)
        xhat = norm.tile([P, LT, PACK, P], F32)
        xT_banks = []
        for half in range(2):
            even_bank = psum.tile([P, 2, HALF], F32, tag="vector_bank", bufs=2, name="xT_even%d" % half)
            odd_bank = psum.tile([P, 2, HALF], F32, tag="scalar_bank", bufs=6, name="xT_odd%d" % half)
            xT_banks.append((even_bank, odd_bank))

        total = norm.tile([P, 1], F32)
        squares = norm.tile([P, 1], F32)
        neg_mean = norm.tile([P, 1], F32)
        waste_sum = norm.tile([P, E], F32)
        waste_squares = norm.tile([P, E], F32)
        std_1 = norm.tile([P, 1], F32)
        rstd_1 = norm.tile([P, 1], F32)
        shift_1 = norm.tile([P, 1], F32)

        def vector_statistics(lt):
            nc.vector.bn_stats(out=stats[:, lt, :], in_=q_sb[:, lt, :])

        def vector_moments(lt):
            nc.vector.bn_aggr(out=mean_var[:, lt, :], in_=stats[:, lt, :])
            nc.scalar.activation(
                out=std[:, lt : lt + 1], in_=mean_var[:, lt, 1:2], func=ACT.Sqrt, bias=eps_t[:, 0:1], scale=1.0
            )

        def vector_shift(lt):
            nc.vector.reciprocal(out=rstd[:, lt : lt + 1], in_=std[:, lt : lt + 1])
            nc.vector.scalar_tensor_tensor(
                out=shift[:, lt : lt + 1], in0=mean_var[:, lt, 0:1], scalar=-1.0, in1=rstd[:, lt : lt + 1],
                op0=ALU.mult, op1=ALU.mult,
            )

        def scalar_sum():
            nc.scalar.activation(out=waste_sum[:], in_=q_sb[:, 1, :], func=ACT.Identity, accum_out=total[:])
            nc.scalar.mul(out=neg_mean[:], in_=total[:], mul=-1.0 / E)

        def scalar_squares():
            nc.scalar.activation(
                out=waste_squares[:], in_=q_sb[:, 1, :], func=ACT.Square, bias=neg_mean[:, 0:1], accum_out=squares[:]
            )
            nc.scalar.activation(out=std_1[:], in_=squares[:], func=ACT.Sqrt, bias=eps_t[:, 0:1], scale=1.0 / E)

        def scalar_shift():
            nc.vector.reciprocal(out=rstd_1[:], in_=std_1[:])
            nc.scalar.activation(out=shift_1[:], in_=neg_mean[:], func=ACT.Copy, scale=rstd_1[:, 0:1])

        def normalise(lt):
            if lt == 1:
                scale, bias = rstd_1[:, 0:1], shift_1[:, 0:1]
            else:
                scale, bias = rstd[:, lt : lt + 1], shift[:, lt : lt + 1]
            nc.scalar.activation(
                out=xhat[:, lt], in_=q_sb[:, lt, :].rearrange("p (j t) -> p t j", t=PACK), func=ACT.Identity,
                scale=scale, bias=bias,
            )
            l_cols = slice((lt % 2) * P, (lt % 2 + 1) * P)
            for t in range(PACK):
                nc.tensor.transpose(out=xT_banks[lt // 2][t % 2][:, t // 2, l_cols], in_=xhat[:, lt, t, :], identity=ident[:])

        x_planes = norm.tile([P, PACK, L], BF16)
        x_grouped = norm.tile([P, L, PACK], BF16, align_bytes=64)
        x_codes = norm.tile([P, L], U32, align_bytes=64)
        x_scales = norm.tile([P, L], U8, align_bytes=64)

        def scale_and_shift(half):
            l_cols = slice(half * HALF, (half + 1) * HALF)
            for t in range(PACK):
                if half == 0 and t % 2 == 0:
                    nc.vector.tensor_scalar(
                        out=x_planes[:, t, l_cols], in0=xT_banks[half][t % 2][:, t // 2, :],
                        scalar1=g_f[:, t : t + 1], scalar2=b_f[:, t : t + 1], op0=ALU.mult, op1=ALU.add,
                    )
                else:
                    nc.scalar.activation(
                        out=x_planes[:, t, l_cols], in_=xT_banks[half][t % 2][:, t // 2, :], func=ACT.Identity,
                        scale=g_f[:, t : t + 1], bias=b_f[:, t : t + 1],
                    )

        def regroup_x(half):
            l_cols = slice(half * HALF, (half + 1) * HALF)
            regroup(nc.vector.tensor_copy, x_grouped[:, l_cols, :], x_planes[:, :, l_cols])

        def quantise_x(half):
            l_cols = slice(half * HALF, (half + 1) * HALF)
            nc.vector.quantize_mx(
                out=x_codes[:, l_cols].bitcast(FP8X4),
                scales=x_scales[:, l_cols],
                in_=x_grouped[:, l_cols, :].rearrange("p l t -> p (l t)"),
            )

        nc.gpsimd.tensor_copy(out=g_f[:], in_=g_bf[:])
        nc.gpsimd.tensor_copy(out=b_f[:], in_=b_bf[:])

        qk_grouped = {}
        qk_codes = {}
        qk_scales = {}

        def take_bank(on_vector, shape, name):
            if on_vector:
                bank = psum.tile(shape, F32, tag="vector_bank", bufs=2, name=name)
            else:
                bank = psum.tile(shape, F32, tag="scalar_bank", bufs=6, name=name)
            return bank

        def project(h, side, lb, on_vector=False):
            if lb == 0:
                qk_grouped[h, side] = qk_pool.tile([P, L, PACK], BF16, align_bytes=64, name="qk_grouped")
                qk_codes[h, side] = qk_pool.tile([P, L], U32, align_bytes=64, name="qk_codes")
                qk_scales[h, side] = qk_pool.tile([P, L], U8, align_bytes=64, name="qk_scales")
            l_cols = slice(lb * P, (lb + 1) * P)
            bank = take_bank(on_vector, [P, PACK, P], "proj_bank")
            for t in range(PACK):
                d_cols = slice(side * D + t * P, side * D + (t + 1) * P)
                nc.tensor.matmul_mx(
                    out=bank[:, t, :],
                    lhsT=w_codes[h][:, d_cols].bitcast(FP8X4),
                    lhsT_scale=w_scales[h][:, d_cols],
                    rhs=x_codes[:, l_cols].bitcast(FP8X4),
                    rhs_scale=x_scales[:, l_cols],
                    start=True,
                    stop=True,
                )
            copy = nc.vector.tensor_copy if on_vector else nc.scalar.copy
            copy(out=qk_grouped[h, side][:, l_cols, :], in_=bank[:].rearrange("p t l -> p l t"))

        def quantise_qk(h, side, half):
            l_cols = slice(half * HALF, (half + 1) * HALF)
            nc.vector.quantize_mx(
                out=qk_codes[h, side][:, l_cols].bitcast(FP8X4),
                scales=qk_scales[h, side][:, l_cols],
                in_=qk_grouped[h, side][:, l_cols, :].rearrange("p l t -> p (l t)"),
            )

        def logits(h, lt, on_vector):
            q_cols = slice(lt * P, (lt + 1) * P)
            bank = take_bank(on_vector, [P, L], "logit_bank")
            nc.tensor.matmul_mx(
                out=bank[:],
                lhsT=qk_codes[h, Q_SIDE][:, q_cols].bitcast(FP8X4),
                lhsT_scale=qk_scales[h, Q_SIDE][:, q_cols],
                rhs=qk_codes[h, K_SIDE][:].bitcast(FP8X4),
                rhs_scale=qk_scales[h, K_SIDE][:],
                start=True,
                stop=True,
            )
            rows = out_pool.tile([P, L], F32, name="out_rows")
            if on_vector:
                nc.vector.tensor_scalar(out=rows[:], in0=bank[:], scalar1=OUT_SCALE, scalar2=None, op0=ALU.mult)
            else:
                nc.scalar.mul(out=rows[:], in_=bank[:], mul=OUT_SCALE)
            nc.sync.dma_start(out=out[0, h, lt * P : (lt + 1) * P, :], in_=rows[:])

        ctx.enter_context(tc.manual_schedule())
        vector_statistics(0)
        scalar_sum()
        vector_moments(0)
        scalar_squares()
        vector_statistics(2)
        vector_shift(0)
        vector_moments(2)
        normalise(0)
        vector_statistics(3)
        scalar_shift()
        normalise(1)
        vector_moments(3)
        vector_shift(2)
        normalise(2)
        regroup_weights(nc.vector.tensor_copy, 0, K_SIDE, first=0, last=1, pieces=2)
        vector_shift(3)
        normalise(3)
        regroup_weights(nc.vector.tensor_copy, 0, K_SIDE, first=1, last=2, pieces=2)
        scale_and_shift(0)
        regroup_x(0)
        quantise_weights(0, K_SIDE, 1)
        quantise_x(0)
        scale_and_shift(1)
        regroup_weights(nc.scalar.copy, 0, Q_SIDE, first=0, last=2, pieces=4)
        project(0, K_SIDE, 0)
        project(0, K_SIDE, 1)
        regroup_x(1)
        regroup_weights(nc.vector.tensor_copy, 0, Q_SIDE, first=2, last=3, pieces=4)
        quantise_x(1)
        regroup_weights(nc.vector.tensor_copy, 0, Q_SIDE, first=3, last=4, pieces=4)
        project(0, K_SIDE, 2)
        project(0, K_SIDE, 3)
        quantise_weights(0, Q_SIDE, 1)
        for lb in range(LT):
            project(0, Q_SIDE, lb)
        regroup_weights(nc.vector.tensor_copy, 1, K_SIDE)
        quantise_qk(0, K_SIDE, 0)
        quantise_weights(1, K_SIDE, 1)
        quantise_qk(0, K_SIDE, 1)
        regroup_weights(nc.vector.tensor_copy, 1, Q_SIDE)
        quantise_qk(0, Q_SIDE, 0)
        quantise_weights(1, Q_SIDE, 1)
        quantise_qk(0, Q_SIDE, 1)

        for h in range(1, H - 1):
            for lb in range(LT):
                project(h, K_SIDE, lb)
            regroup_weights(nc.vector.tensor_copy, h + 1, K_SIDE)
            quantise_qk(h, K_SIDE, 0)
            quantise_weights(h + 1, K_SIDE, 1)
            quantise_qk(h, K_SIDE, 1)
            for lb in range(LT):
                project(h, Q_SIDE, lb)
            regroup_weights(nc.vector.tensor_copy, h + 1, Q_SIDE)
            quantise_qk(h, Q_SIDE, 0)
            quantise_weights(h + 1, Q_SIDE, 1)
            quantise_qk(h, Q_SIDE, 1)
            for lt in range(LT):
                logits(h - 1, lt, lt == 3 or (lt == 1 and h > 1))

        for lb in range(LT):
            project(H - 1, K_SIDE, lb)
        quantise_qk(H - 1, K_SIDE, 0)
        quantise_qk(H - 1, K_SIDE, 1)
        for lt in (0, 1):
            logits(H - 2, lt, lt == 1)

        for lb in range(LT):
            project(H - 1, Q_SIDE, lb, on_vector=lb % 2 == 1)
            if lb % 2 == 1:
                quantise_qk(H - 1, Q_SIDE, lb // 2)
        for lt in (2, 3):
            logits(H - 2, lt, False)
        for lt in range(LT):
            logits(H - 1, lt, lt % 2 == 1)
